import numpy as np
import ml_dtypes


def mxq(x, axis, fmt="e4m3"):
    dtype, down = {"e4m3": (ml_dtypes.float8_e4m3fn, 7), "e5m2": (ml_dtypes.float8_e5m2, 14)}[fmt]
    v = np.moveaxis(np.asarray(x, np.float32).astype(ml_dtypes.bfloat16).astype(np.float64), axis, -1)
    blocks = v.reshape(v.shape[:-1] + (-1, 32))
    amax = np.abs(blocks).max(-1, keepdims=True)
    byte = np.maximum(np.where(amax > 0, np.frexp(amax)[1] - 1 + 127, 0) - down, 1)
    scale = np.exp2(byte - 127.0)
    codes = (blocks / scale).astype(np.float32).astype(dtype).astype(np.float64)
    return np.moveaxis((codes * scale).reshape(v.shape), -1, axis)


WIDE = False


def mx_kscale(k):
    if not WIDE:
        return np.ones(k)
    levels = np.array([10, -10, 5, -5, 0])
    a = np.random.permutation(np.resize(levels, k // 512 * 4)).reshape(k // 512, 4)
    idx = np.arange(k)
    return np.exp2(a[idx // 512, idx % 128 // 32])


BF16 = ml_dtypes.bfloat16


def bf(x):
    return np.asarray(x, np.float32).astype(BF16)


def f64(x):
    return np.asarray(x).astype(np.float64)


B, S, IN, OUT, R, RT = 4, 2048, 1024, 512, 512, 64


def setup_inputs():
    r, t = mx_kscale(R), mx_kscale(IN)
    return {
        "x": bf(np.random.standard_normal((B, S, IN)) * t),
        "siva_u_t": bf(np.random.standard_normal((OUT, RT)) * 1.7 / np.sqrt(R) * r[:RT]),
        "siva_u_d": bf(np.random.standard_normal((OUT, R - RT)) * 1.7 / np.sqrt(R) * r[RT:]),
        "siva_s": bf(np.random.uniform(0.0, 1.0, R)),
        "siva_v_t": bf(np.random.standard_normal((RT, IN)) / np.sqrt(IN) / r[:RT, None] / t),
        "siva_v_d": bf(np.random.standard_normal((R - RT, IN)) / np.sqrt(IN) / r[RT:, None] / t),
        "bias": bf(np.random.standard_normal(OUT) * 0.5),
    }


def reference(x, siva_u_t, siva_u_d, siva_s, siva_v_t, siva_v_d, bias):
    siva_u = np.concatenate((f64(siva_u_t), f64(siva_u_d)), axis=1)
    siva_v = np.concatenate((f64(siva_v_t), f64(siva_v_d)), axis=0)
    weight = mxq(siva_u * f64(siva_s), 1, "e4m3") @ mxq(siva_v, 0, "e4m3")
    return (mxq(f64(x), 2, "e4m3") @ mxq(weight, 1, "e4m3").T) + f64(bias)

@@ -1,0 +1,227 @@
+from contextlib import ExitStack
+
+import concourse.masks as masks
+import concourse.mybir as mybir
+
+BF16 = mybir.dt.bfloat16
+F32 = mybir.dt.float32
+I32 = mybir.dt.int32
+U32 = mybir.dt.uint32
+U8 = mybir.dt.uint8
+FP8X4 = mybir.dt.float8_e4m3fn_x4
+ADD = mybir.AluOpType.add
+MULT = mybir.AluOpType.mult
+
+P = 128
+TOKENS = 8192
+IN = 1024
+OUT = 512
+R = 512
+RT = 64
+SLOTS = 4
+GROUPS = TOKENS // (P * SLOTS)
+FLOPS = 2 * OUT * R * IN + 2 * TOKENS * IN * OUT
+
+RX = 10
+NG = 3
+NC = 4
+NO = 4
+
+
+def tile_sivalinear_t_kernel(
+    tc, x, siva_u_t, siva_u_d, siva_s, siva_v_t, siva_v_d, bias, out
+):
+    nc = tc.nc
+    xg = x.flatten_outer_dims().rearrange("(i p s) k -> i p (s k)", p=P, s=SLOTS)
+    og = out.flatten_outer_dims().rearrange("(i p s) n -> i p (s n)", p=P, s=SLOTS)
+
+    with ExitStack() as ctx:
+        const = ctx.enter_context(tc.tile_pool(name="const", bufs=1))
+        xpool = ctx.enter_context(tc.tile_pool(name="xpool", bufs=1))
+        gpool = ctx.enter_context(tc.tile_pool(name="gpool", bufs=1))
+        cpool = ctx.enter_context(tc.tile_pool(name="cpool", bufs=1))
+        opool = ctx.enter_context(tc.tile_pool(name="opool", bufs=1))
+        psum = ctx.enter_context(tc.psum_pool(name="psum", bufs=1))
+        ctx.enter_context(tc.manual_schedule())
+
+        rows = const.tile([P, R + OUT], BF16, name="rows")
+        ones = const.tile([P, P], BF16, name="ones")
+        ident_b = const.tile([P, P], BF16, name="ident_b")
+        ident_f = const.tile([P, P], F32, name="ident_f")
+        nc.vector.memset(rows[:].bitcast(I32), 0)
+        nc.vector.memset(ones[:], 1.0)
+        masks.make_identity(nc, ident_b[:])
+        masks.make_identity(nc, ident_f[:])
+
+        u_sb = const.tile([P, 4, R], BF16, name="u_sb")
+        v_sb = const.tile([P, 4, IN], BF16, name="v_sb")
+        nc.sync.dma_start(out=u_sb[:, :, RT:R], in_=siva_u_d.rearrange("(o p) r -> p o r", p=P))
+        nc.sync.dma_start(out=u_sb[:, :, 0:RT], in_=siva_u_t.rearrange("(o p) r -> p o r", p=P))
+        nc.scalar.dma_start(out=rows[0:1, 0:R], in_=siva_s.rearrange("(o n) -> o n", o=1))
+        nc.scalar.dma_start(out=rows[0:1, R : R + OUT], in_=bias.rearrange("(o n) -> o n", o=1))
+        nc.sync.dma_start(out=v_sb[0:RT, 0, :], in_=siva_v_t)
+        nc.sync.dma_start(out=v_sb[RT:P, 0, :], in_=siva_v_d[0 : P - RT, :])
+        nc.sync.dma_start(
+            out=v_sb[:, 1:4, :], in_=siva_v_d[P - RT :, :].rearrange("(j q) c -> q j c", q=P)
+        )
+
+        xs = {}
+
+        def load_x(i):
+            t = xpool.tile([P, SLOTS * IN], BF16, name="xs", tag="xs%d" % (i % RX))
+            nc.sync.dma_start(out=t[:], in_=xg[i])
+            xs[i] = t
+
+        for i in range(RX):
+            load_x(i)
+
+        ps_s = psum.tile([P, R], F32, name="ps_s", tag="acc0")
+        ps_b = psum.tile([P, OUT], F32, name="ps_b", tag="acc1")
+        nc.tensor.matmul(out=ps_s[:], lhsT=ones[:], rhs=rows[:, 0:R], start=True, stop=True)
+        nc.tensor.matmul(out=ps_b[:], lhsT=ones[:], rhs=rows[:, R : R + OUT], start=True, stop=True)
+        s_bc = const.tile([P, R], BF16, name="s_bc")
+        bias_bc = const.tile([P, OUT], F32, name="bias_bc")
+        nc.scalar.copy(out=s_bc[:], in_=ps_s[:])
+        nc.scalar.copy(out=bias_bc[:], in_=ps_b[:])
+
+        us = const.tile([P, 4, R], BF16, name="us")
+        gu = const.tile([P, OUT, 4], BF16, name="gu", align_bytes=64)
+        for o in range(4):
+            nc.vector.tensor_tensor(out=us[:, o, :], in0=u_sb[:, o, :], in1=s_bc[:], op=MULT)
+            ut = psum.tile([P, 4, P], BF16, name="ut", tag="acc%d" % ((o + 2) % 4))
+            for t in range(4):
+                nc.tensor.transpose(ut[:, t, :], us[:, o, t * P : (t + 1) * P], ident_b[:])
+            nc.scalar.copy(
+                out=gu[:, o * P : (o + 1) * P, :], in_=ut[:].rearrange("p t c -> p c t")
+            )
+
+        gv = const.tile([P, IN, 4], BF16, name="gv", align_bytes=64)
+
+        def regroup_v(a, eng_copy):
+            eng_copy(
+                out=gv[:, a * 256 : (a + 1) * 256, :].rearrange("q (e p) j -> q e p j", e=2),
+                in_=v_sb[:, :, a * 256 : (a + 1) * 256].rearrange("q j (p e) -> q e p j", e=2),
+            )
+
+        u_codes = const.tile([P, OUT], U32, name="u_codes", align_bytes=64)
+        u_scales = const.tile([P, OUT], U8, name="u_scales", align_bytes=64)
+        v_codes = const.tile([P, IN], U32, name="v_codes", align_bytes=64)
+        v_scales = const.tile([P, IN], U8, name="v_scales", align_bytes=64)
+
+        def quant_v(g):
+            nc.vector.quantize_mx(
+                out=v_codes[:, g * 512 : (g + 1) * 512].bitcast(FP8X4),
+                scales=v_scales[:, g * 512 : (g + 1) * 512],
+                in_=gv[:, g * 512 : (g + 1) * 512, :].rearrange("q c j -> q (c j)"),
+            )
+
+        regroup_v(0, nc.vector.tensor_copy)
+        regroup_v(1, nc.vector.tensor_copy)
+        regroup_v(3, nc.scalar.copy)
+        nc.vector.quantize_mx(
+            out=u_codes[:].bitcast(FP8X4),
+            scales=u_scales[:],
+            in_=gu[:].rearrange("p n t -> p (n t)"),
+        )
+        quant_v(0)
+        regroup_v(2, nc.vector.tensor_copy)
+        quant_v(1)
+
+        gw = const.tile([P, 2, OUT, 4], BF16, name="gw", align_bytes=64)
+        w_codes = const.tile([P, 2 * OUT], U32, name="w_codes", align_bytes=64)
+        w_scales = const.tile([P, 2 * OUT], U8, name="w_scales", align_bytes=64)
+
+        def weight_half(g):
+            for c in range(4):
+                wt = psum.tile([P, 4, P], F32, name="wt", tag="acc%d" % c)
+                for t in range(4):
+                    m = (4 * g + t) * P
+                    nc.tensor.matmul_mx(
+                        out=wt[:, t, :],
+                        lhsT=v_codes[:, m : m + P].bitcast(FP8X4),
+                        lhsT_scale=v_scales[:, m : m + P],
+                        rhs=u_codes[:, c * P : (c + 1) * P].bitcast(FP8X4),
+                        rhs_scale=u_scales[:, c * P : (c + 1) * P],
+                        start=True,
+                        stop=True,
+                    )
+                eng_copy = nc.vector.tensor_copy if c % 2 == 0 else nc.scalar.copy
+                eng_copy(
+                    out=gw[:, g, c * P : (c + 1) * P, :], in_=wt[:].rearrange("p t c -> p c t")
+                )
+
+        def quant_w(g):
+            nc.vector.quantize_mx(
+                out=w_codes[:, g * OUT : (g + 1) * OUT].bitcast(FP8X4),
+                scales=w_scales[:, g * OUT : (g + 1) * OUT],
+                in_=gw[:, g].rearrange("p n t -> p (n t)"),
+            )
+
+        gxs = {}
+        codes = {}
+
+        def transposes(i):
+            xw = xs[i][:].bitcast(F32)
+            gx = gpool.tile([P, SLOTS * IN], BF16, name="gx", tag="gx%d" % (i % NG), align_bytes=64)
+            g32 = gx[:].bitcast(F32).rearrange("p (s g r u) -> p s g r u", s=SLOTS, g=2, r=P, u=2)
+            banks = []
+            for s in range(SLOTS):
+                xt = psum.tile([P, 4, P], F32, name="xt", tag="xt%d" % s)
+                for a in range(4):
+                    w0 = s * 512 + a * P
+                    nc.tensor.transpose(xt[:, a, :], xw[:, w0 : w0 + P], ident_f[:])
+                banks.append(xt)
+            for s in range(SLOTS):
+                nc.scalar.copy(out=g32[:, s], in_=banks[s][:].rearrange("p (g u) r -> p g r u", u=2))
+            gxs[i] = gx
+            if i + RX < GROUPS:
+                load_x(i + RX)
+
+        def quant_x(i):
+            xc = cpool.tile([P, SLOTS * 2 * P], U32, name="xc", tag="xc%d" % (i % NC), align_bytes=64)
+            xsc = cpool.tile([P, SLOTS * 2 * P], U8, name="xsc", tag="xsc%d" % (i % NC), align_bytes=64)
+            nc.vector.quantize_mx(out=xc[:].bitcast(FP8X4), scales=xsc[:], in_=gxs[i][:])
+            codes[i] = (xc, xsc)
+
+        def multiply(i):
+            xc, xsc = codes[i]
+            ost = opool.tile([P, SLOTS * OUT], F32, name="ost", tag="ost%d" % (i % NO))
+            accs = []
+            for s in range(SLOTS):
+                acc = psum.tile([P, OUT], F32, name="acc", tag="acc%d" % s)
+                for g in range(2):
+                    c0 = (s * 2 + g) * P
+                    nc.tensor.matmul_mx(
+                        out=acc[:],
+                        lhsT=xc[:, c0 : c0 + P].bitcast(FP8X4),
+                        lhsT_scale=xsc[:, c0 : c0 + P],
+                        rhs=w_codes[:, g * OUT : (g + 1) * OUT].bitcast(FP8X4),
+                        rhs_scale=w_scales[:, g * OUT : (g + 1) * OUT],
+                        start=(g == 0),
+                        stop=(g == 1),
+                    )
+                accs.append(acc)
+            for s in range(SLOTS):
+                nc.vector.tensor_tensor(
+                    out=ost[:, s * OUT : (s + 1) * OUT], in0=accs[s][:], in1=bias_bc[:], op=ADD
+                )
+            if i < GROUPS - 1:
+                nc.gpsimd.dma_start(out=og[i], in_=ost[:])
+            else:
+                nc.sync.dma_start(out=og[i][:, 0 : 2 * OUT], in_=ost[:, 0 : 2 * OUT])
+                nc.sync.dma_start(out=og[i][:, 2 * OUT :], in_=ost[:, 2 * OUT :])
+
+        weight_half(0)
+        transposes(0)
+        weight_half(1)
+        quant_w(0)
+        transposes(1)
+        quant_x(0)
+        quant_w(1)
+        quant_x(1)
+        for j in range(2, GROUPS + 2):
+            if j < GROUPS:
+                transposes(j)
+            multiply(j - 2)
+            if j < GROUPS:
+                quant_x(j)

@@ -26,6 +26,7 @@ RX = 10
 NG = 3
 NC = 4
 NO = 4
+ESC = (0,)
 
 
 def tile_sivalinear_t_kernel(
@@ -202,9 +203,12 @@ def tile_sivalinear_t_kernel(
                     )
                 accs.append(acc)
             for s in range(SLOTS):
-                nc.vector.tensor_tensor(
-                    out=ost[:, s * OUT : (s + 1) * OUT], in0=accs[s][:], in1=bias_bc[:], op=ADD
-                )
+                dst = ost[:, s * OUT : (s + 1) * OUT]
+                if s in ESC:
+                    nc.scalar.copy(out=dst, in_=accs[s][:])
+                    nc.gpsimd.tensor_tensor(out=dst, in0=dst, in1=bias_bc[:], op=ADD)
+                else:
+                    nc.vector.tensor_tensor(out=dst, in0=accs[s][:], in1=bias_bc[:], op=ADD)
             if i < GROUPS - 1:
                 nc.gpsimd.dma_start(out=og[i], in_=ost[:])
             else:

@@ -26,7 +26,7 @@ RX = 10
 NG = 3
 NC = 4
 NO = 4
-ESC = (0,)
+FINE = 13
 
 
 def tile_sivalinear_t_kernel(
@@ -45,55 +45,73 @@ def tile_sivalinear_t_kernel(
         psum = ctx.enter_context(tc.psum_pool(name="psum", bufs=1))
         ctx.enter_context(tc.manual_schedule())
 
-        rows = const.tile([P, R + OUT], BF16, name="rows")
+        rows = const.tile([P, OUT], BF16, name="rows")
         ones = const.tile([P, P], BF16, name="ones")
-        ident_b = const.tile([P, P], BF16, name="ident_b")
         ident_f = const.tile([P, P], F32, name="ident_f")
         nc.vector.memset(rows[:].bitcast(I32), 0)
         nc.vector.memset(ones[:], 1.0)
-        masks.make_identity(nc, ident_b[:])
         masks.make_identity(nc, ident_f[:])
 
-        u_sb = const.tile([P, 4, R], BF16, name="u_sb")
+        s_col = const.tile([P, 4], BF16, name="s_col")
+        u_sb = const.tile([P, 4 * R], BF16, name="u_sb")
         v_sb = const.tile([P, 4, IN], BF16, name="v_sb")
-        nc.sync.dma_start(out=u_sb[:, :, RT:R], in_=siva_u_d.rearrange("(o p) r -> p o r", p=P))
-        nc.sync.dma_start(out=u_sb[:, :, 0:RT], in_=siva_u_t.rearrange("(o p) r -> p o r", p=P))
-        nc.scalar.dma_start(out=rows[0:1, 0:R], in_=siva_s.rearrange("(o n) -> o n", o=1))
-        nc.scalar.dma_start(out=rows[0:1, R : R + OUT], in_=bias.rearrange("(o n) -> o n", o=1))
-        nc.sync.dma_start(out=v_sb[0:RT, 0, :], in_=siva_v_t)
-        nc.sync.dma_start(out=v_sb[RT:P, 0, :], in_=siva_v_d[0 : P - RT, :])
+        u3 = u_sb[:].rearrange("p (o r) -> p o r", o=4)
         nc.sync.dma_start(
-            out=v_sb[:, 1:4, :], in_=siva_v_d[P - RT :, :].rearrange("(j q) c -> q j c", q=P)
+            out=s_col[:].rearrange("q (a e) -> q a e", a=2),
+            in_=siva_s.rearrange("(a q e) -> q a e", a=2, e=2),
         )
+        nc.sync.dma_start(out=u3[:, :, RT:R], in_=siva_u_d.rearrange("(o p) r -> p o r", p=P))
+        nc.sync.dma_start(out=u3[:, :, 0:RT], in_=siva_u_t.rearrange("(o p) r -> p o r", p=P))
+        nc.scalar.dma_start(out=rows[0:1, :], in_=bias.rearrange("(o n) -> o n", o=1))
+        qt = RT // 2
+        nc.sync.dma_start(
+            out=v_sb[:, 2:4, :],
+            in_=siva_v_d[256 - RT :, :].rearrange("(q e) c -> q e c", e=2),
+        )
+        nc.sync.dma_start(
+            out=v_sb[qt:P, 0:2, :],
+            in_=siva_v_d[0 : 256 - RT, :].rearrange("(q e) c -> q e c", e=2),
+        )
+        nc.sync.dma_start(out=v_sb[0:qt, 0:2, :], in_=siva_v_t.rearrange("(q e) c -> q e c", e=2))
 
         xs = {}
 
-        def load_x(i):
+        def load_x(i, pieces):
             t = xpool.tile([P, SLOTS * IN], BF16, name="xs", tag="xs%d" % (i % RX))
-            nc.sync.dma_start(out=t[:], in_=xg[i])
+            w = SLOTS * IN // pieces
+            for h in range(pieces):
+                nc.sync.dma_start(out=t[:, h * w : (h + 1) * w], in_=xg[i][:, h * w : (h + 1) * w])
             xs[i] = t
 
-        for i in range(RX):
-            load_x(i)
+        load_x(0, 2)
+        for i in range(1, RX):
+            load_x(i, 1)
 
-        ps_s = psum.tile([P, R], F32, name="ps_s", tag="acc0")
-        ps_b = psum.tile([P, OUT], F32, name="ps_b", tag="acc1")
-        nc.tensor.matmul(out=ps_s[:], lhsT=ones[:], rhs=rows[:, 0:R], start=True, stop=True)
-        nc.tensor.matmul(out=ps_b[:], lhsT=ones[:], rhs=rows[:, R : R + OUT], start=True, stop=True)
-        s_bc = const.tile([P, R], BF16, name="s_bc")
+        gu = const.tile([P, OUT, 4], BF16, name="gu", align_bytes=64)
+        uw = u_sb[:].bitcast(F32)
+        s_b = s_col[:].rearrange("q (a e) -> q a e", a=2).unsqueeze(1).to_broadcast([P, P, 2, 2])
+        utbs = []
+        for b in range(2):
+            utb = psum.tile([P, 4 * P], F32, name="utb", tag="acc%d" % b)
+            for k in range(4):
+                w0 = (2 * b + k // 2) * 256 + (k % 2) * P
+                nc.tensor.transpose(utb[:, k * P : (k + 1) * P], uw[:, w0 : w0 + P], ident_f[:])
+            utbs.append(utb)
+
+        ps_b = psum.tile([P, OUT], F32, name="ps_b", tag="acc2")
+        nc.tensor.matmul(out=ps_b[:], lhsT=ones[:], rhs=rows[:], start=True, stop=True)
         bias_bc = const.tile([P, OUT], F32, name="bias_bc")
-        nc.scalar.copy(out=s_bc[:], in_=ps_s[:])
         nc.scalar.copy(out=bias_bc[:], in_=ps_b[:])
 
-        us = const.tile([P, 4, R], BF16, name="us")
-        gu = const.tile([P, OUT, 4], BF16, name="gu", align_bytes=64)
         for o in range(4):
-            nc.vector.tensor_tensor(out=us[:, o, :], in0=u_sb[:, o, :], in1=s_bc[:], op=MULT)
-            ut = psum.tile([P, 4, P], BF16, name="ut", tag="acc%d" % ((o + 2) % 4))
-            for t in range(4):
-                nc.tensor.transpose(ut[:, t, :], us[:, o, t * P : (t + 1) * P], ident_b[:])
-            nc.scalar.copy(
-                out=gu[:, o * P : (o + 1) * P, :], in_=ut[:].rearrange("p t c -> p c t")
+            u16 = utbs[o // 2][:].bitcast(BF16).rearrange(
+                "p (o a n e) -> p o a n e", o=2, a=2, n=P, e=2
+            )
+            nc.vector.tensor_tensor(
+                out=gu[:, o * P : (o + 1) * P, :].rearrange("p n (a e) -> p n a e", a=2),
+                in0=u16[:, o % 2].rearrange("p a n e -> p n a e"),
+                in1=s_b,
+                op=MULT,
             )
 
         gv = const.tile([P, IN, 4], BF16, name="gv", align_bytes=64)
@@ -116,16 +134,16 @@ def tile_sivalinear_t_kernel(
                 in_=gv[:, g * 512 : (g + 1) * 512, :].rearrange("q c j -> q (c j)"),
             )
 
+        regroup_v(2, nc.scalar.copy)
+        regroup_v(3, nc.scalar.copy)
         regroup_v(0, nc.vector.tensor_copy)
         regroup_v(1, nc.vector.tensor_copy)
-        regroup_v(3, nc.scalar.copy)
         nc.vector.quantize_mx(
             out=u_codes[:].bitcast(FP8X4),
             scales=u_scales[:],
             in_=gu[:].rearrange("p n t -> p (n t)"),
         )
         quant_v(0)
-        regroup_v(2, nc.vector.tensor_copy)
         quant_v(1)
 
         gw = const.tile([P, 2, OUT, 4], BF16, name="gw", align_bytes=64)
@@ -176,12 +194,18 @@ def tile_sivalinear_t_kernel(
                 nc.scalar.copy(out=g32[:, s], in_=banks[s][:].rearrange("p (g u) r -> p g r u", u=2))
             gxs[i] = gx
             if i + RX < GROUPS:
-                load_x(i + RX)
+                load_x(i + RX, 1)
 
-        def quant_x(i):
+        def quant_x(i, pieces):
             xc = cpool.tile([P, SLOTS * 2 * P], U32, name="xc", tag="xc%d" % (i % NC), align_bytes=64)
             xsc = cpool.tile([P, SLOTS * 2 * P], U8, name="xsc", tag="xsc%d" % (i % NC), align_bytes=64)
-            nc.vector.quantize_mx(out=xc[:].bitcast(FP8X4), scales=xsc[:], in_=gxs[i][:])
+            w = SLOTS * 2 * P // pieces
+            for h in range(pieces):
+                nc.vector.quantize_mx(
+                    out=xc[:, h * w : (h + 1) * w].bitcast(FP8X4),
+                    scales=xsc[:, h * w : (h + 1) * w],
+                    in_=gxs[i][:, 4 * h * w : 4 * (h + 1) * w],
+                )
             codes[i] = (xc, xsc)
 
         def multiply(i):
@@ -203,29 +227,24 @@ def tile_sivalinear_t_kernel(
                     )
                 accs.append(acc)
             for s in range(SLOTS):
-                dst = ost[:, s * OUT : (s + 1) * OUT]
-                if s in ESC:
-                    nc.scalar.copy(out=dst, in_=accs[s][:])
-                    nc.gpsimd.tensor_tensor(out=dst, in0=dst, in1=bias_bc[:], op=ADD)
-                else:
-                    nc.vector.tensor_tensor(out=dst, in0=accs[s][:], in1=bias_bc[:], op=ADD)
-            if i < GROUPS - 1:
+                cols = slice(s * OUT, (s + 1) * OUT)
+                nc.vector.tensor_tensor(out=ost[:, cols], in0=accs[s][:], in1=bias_bc[:], op=ADD)
+                if i >= FINE:
+                    nc.sync.dma_start(out=og[i][:, cols], in_=ost[:, cols])
+            if i < FINE:
                 nc.gpsimd.dma_start(out=og[i], in_=ost[:])
-            else:
-                nc.sync.dma_start(out=og[i][:, 0 : 2 * OUT], in_=ost[:, 0 : 2 * OUT])
-                nc.sync.dma_start(out=og[i][:, 2 * OUT :], in_=ost[:, 2 * OUT :])
 
-        weight_half(0)
         transposes(0)
+        weight_half(0)
         weight_half(1)
         quant_w(0)
         transposes(1)
-        quant_x(0)
         quant_w(1)
-        quant_x(1)
+        quant_x(0, 4)
+        quant_x(1, 1)
         for j in range(2, GROUPS + 2):
             if j < GROUPS:
                 transposes(j)
             multiply(j - 2)
             if j < GROUPS:
-                quant_x(j)
+                quant_x(j, 1)

from contextlib import ExitStack

import concourse.masks as masks
import concourse.mybir as mybir

BF16 = mybir.dt.bfloat16
F32 = mybir.dt.float32
I32 = mybir.dt.int32
U32 = mybir.dt.uint32
U8 = mybir.dt.uint8
FP8X4 = mybir.dt.float8_e4m3fn_x4
ADD = mybir.AluOpType.add
MULT = mybir.AluOpType.mult

P = 128
TOKENS = 8192
IN = 1024
OUT = 512
R = 512
RT = 64
SLOTS = 4
GROUPS = TOKENS // (P * SLOTS)
FLOPS = 2 * OUT * R * IN + 2 * TOKENS * IN * OUT

RX = 10
NG = 3
NC = 4
NO = 4
FINE = 13


def tile_sivalinear_t_kernel(
    tc, x, siva_u_t, siva_u_d, siva_s, siva_v_t, siva_v_d, bias, out
):
    nc = tc.nc
    xg = x.flatten_outer_dims().rearrange("(i p s) k -> i p (s k)", p=P, s=SLOTS)
    og = out.flatten_outer_dims().rearrange("(i p s) n -> i p (s n)", p=P, s=SLOTS)

    with ExitStack() as ctx:
        const = ctx.enter_context(tc.tile_pool(name="const", bufs=1))
        xpool = ctx.enter_context(tc.tile_pool(name="xpool", bufs=1))
        gpool = ctx.enter_context(tc.tile_pool(name="gpool", bufs=1))
        cpool = ctx.enter_context(tc.tile_pool(name="cpool", bufs=1))
        opool = ctx.enter_context(tc.tile_pool(name="opool", bufs=1))
        psum = ctx.enter_context(tc.psum_pool(name="psum", bufs=1))
        ctx.enter_context(tc.manual_schedule())

        rows = const.tile([P, OUT], BF16, name="rows")
        ones = const.tile([P, P], BF16, name="ones")
        ident_f = const.tile([P, P], F32, name="ident_f")
        nc.vector.memset(rows[:].bitcast(I32), 0)
        nc.vector.memset(ones[:], 1.0)
        masks.make_identity(nc, ident_f[:])

        s_col = const.tile([P, 4], BF16, name="s_col")
        u_sb = const.tile([P, 4 * R], BF16, name="u_sb")
        v_sb = const.tile([P, 4, IN], BF16, name="v_sb")
        u3 = u_sb[:].rearrange("p (o r) -> p o r", o=4)
        nc.sync.dma_start(
            out=s_col[:].rearrange("q (a e) -> q a e", a=2),
            in_=siva_s.rearrange("(a q e) -> q a e", a=2, e=2),
        )
        nc.sync.dma_start(out=u3[:, :, RT:R], in_=siva_u_d.rearrange("(o p) r -> p o r", p=P))
        nc.sync.dma_start(out=u3[:, :, 0:RT], in_=siva_u_t.rearrange("(o p) r -> p o r", p=P))
        nc.scalar.dma_start(out=rows[0:1, :], in_=bias.rearrange("(o n) -> o n", o=1))
        qt = RT // 2
        nc.sync.dma_start(
            out=v_sb[:, 2:4, :],
            in_=siva_v_d[256 - RT :, :].rearrange("(q e) c -> q e c", e=2),
        )
        nc.sync.dma_start(
            out=v_sb[qt:P, 0:2, :],
            in_=siva_v_d[0 : 256 - RT, :].rearrange("(q e) c -> q e c", e=2),
        )
        nc.sync.dma_start(out=v_sb[0:qt, 0:2, :], in_=siva_v_t.rearrange("(q e) c -> q e c", e=2))

        xs = {}

        def load_x(i, pieces):
            t = xpool.tile([P, SLOTS * IN], BF16, name="xs", tag="xs%d" % (i % RX))
            w = SLOTS * IN // pieces
            for h in range(pieces):
                nc.sync.dma_start(out=t[:, h * w : (h + 1) * w], in_=xg[i][:, h * w : (h + 1) * w])
            xs[i] = t

        load_x(0, 2)
        for i in range(1, RX):
            load_x(i, 1)

        gu = const.tile([P, OUT, 4], BF16, name="gu", align_bytes=64)
        uw = u_sb[:].bitcast(F32)
        s_b = s_col[:].rearrange("q (a e) -> q a e", a=2).unsqueeze(1).to_broadcast([P, P, 2, 2])
        utbs = []
        for b in range(2):
            utb = psum.tile([P, 4 * P], F32, name="utb", tag="acc%d" % b)
            for k in range(4):
                w0 = (2 * b + k // 2) * 256 + (k % 2) * P
                nc.tensor.transpose(utb[:, k * P : (k + 1) * P], uw[:, w0 : w0 + P], ident_f[:])
            utbs.append(utb)

        ps_b = psum.tile([P, OUT], F32, name="ps_b", tag="acc2")
        nc.tensor.matmul(out=ps_b[:], lhsT=ones[:], rhs=rows[:], start=True, stop=True)
        bias_bc = const.tile([P, OUT], F32, name="bias_bc")
        nc.scalar.copy(out=bias_bc[:], in_=ps_b[:])

        for o in range(4):
            u16 = utbs[o // 2][:].bitcast(BF16).rearrange(
                "p (o a n e) -> p o a n e", o=2, a=2, n=P, e=2
            )
            nc.vector.tensor_tensor(
                out=gu[:, o * P : (o + 1) * P, :].rearrange("p n (a e) -> p n a e", a=2),
                in0=u16[:, o % 2].rearrange("p a n e -> p n a e"),
                in1=s_b,
                op=MULT,
            )

        gv = const.tile([P, IN, 4], BF16, name="gv", align_bytes=64)

        def regroup_v(a, eng_copy):
            eng_copy(
                out=gv[:, a * 256 : (a + 1) * 256, :].rearrange("q (e p) j -> q e p j", e=2),
                in_=v_sb[:, :, a * 256 : (a + 1) * 256].rearrange("q j (p e) -> q e p j", e=2),
            )

        u_codes = const.tile([P, OUT], U32, name="u_codes", align_bytes=64)
        u_scales = const.tile([P, OUT], U8, name="u_scales", align_bytes=64)
        v_codes = const.tile([P, IN], U32, name="v_codes", align_bytes=64)
        v_scales = const.tile([P, IN], U8, name="v_scales", align_bytes=64)

        def quant_v(g):
            nc.vector.quantize_mx(
                out=v_codes[:, g * 512 : (g + 1) * 512].bitcast(FP8X4),
                scales=v_scales[:, g * 512 : (g + 1) * 512],
                in_=gv[:, g * 512 : (g + 1) * 512, :].rearrange("q c j -> q (c j)"),
            )

        regroup_v(2, nc.scalar.copy)
        regroup_v(3, nc.scalar.copy)
        regroup_v(0, nc.vector.tensor_copy)
        regroup_v(1, nc.vector.tensor_copy)
        nc.vector.quantize_mx(
            out=u_codes[:].bitcast(FP8X4),
            scales=u_scales[:],
            in_=gu[:].rearrange("p n t -> p (n t)"),
        )
        quant_v(0)
        quant_v(1)

        gw = const.tile([P, 2, OUT, 4], BF16, name="gw", align_bytes=64)
        w_codes = const.tile([P, 2 * OUT], U32, name="w_codes", align_bytes=64)
        w_scales = const.tile([P, 2 * OUT], U8, name="w_scales", align_bytes=64)

        def weight_half(g):
            for c in range(4):
                wt = psum.tile([P, 4, P], F32, name="wt", tag="acc%d" % c)
                for t in range(4):
                    m = (4 * g + t) * P
                    nc.tensor.matmul_mx(
                        out=wt[:, t, :],
                        lhsT=v_codes[:, m : m + P].bitcast(FP8X4),
                        lhsT_scale=v_scales[:, m : m + P],
                        rhs=u_codes[:, c * P : (c + 1) * P].bitcast(FP8X4),
                        rhs_scale=u_scales[:, c * P : (c + 1) * P],
                        start=True,
                        stop=True,
                    )
                eng_copy = nc.vector.tensor_copy if c % 2 == 0 else nc.scalar.copy
                eng_copy(
                    out=gw[:, g, c * P : (c + 1) * P, :], in_=wt[:].rearrange("p t c -> p c t")
                )

        def quant_w(g):
            nc.vector.quantize_mx(
                out=w_codes[:, g * OUT : (g + 1) * OUT].bitcast(FP8X4),
                scales=w_scales[:, g * OUT : (g + 1) * OUT],
                in_=gw[:, g].rearrange("p n t -> p (n t)"),
            )

        gxs = {}
        codes = {}

        def transposes(i):
            xw = xs[i][:].bitcast(F32)
            gx = gpool.tile([P, SLOTS * IN], BF16, name="gx", tag="gx%d" % (i % NG), align_bytes=64)
            g32 = gx[:].bitcast(F32).rearrange("p (s g r u) -> p s g r u", s=SLOTS, g=2, r=P, u=2)
            banks = []
            for s in range(SLOTS):
                xt = psum.tile([P, 4, P], F32, name="xt", tag="xt%d" % s)
                for a in range(4):
                    w0 = s * 512 + a * P
                    nc.tensor.transpose(xt[:, a, :], xw[:, w0 : w0 + P], ident_f[:])
                banks.append(xt)
            for s in range(SLOTS):
                nc.scalar.copy(out=g32[:, s], in_=banks[s][:].rearrange("p (g u) r -> p g r u", u=2))
            gxs[i] = gx
            if i + RX < GROUPS:
                load_x(i + RX, 1)

        def quant_x(i, pieces):
            xc = cpool.tile([P, SLOTS * 2 * P], U32, name="xc", tag="xc%d" % (i % NC), align_bytes=64)
            xsc = cpool.tile([P, SLOTS * 2 * P], U8, name="xsc", tag="xsc%d" % (i % NC), align_bytes=64)
            w = SLOTS * 2 * P // pieces
            for h in range(pieces):
                nc.vector.quantize_mx(
                    out=xc[:, h * w : (h + 1) * w].bitcast(FP8X4),
                    scales=xsc[:, h * w : (h + 1) * w],
                    in_=gxs[i][:, 4 * h * w : 4 * (h + 1) * w],
                )
            codes[i] = (xc, xsc)

        def multiply(i):
            xc, xsc = codes[i]
            ost = opool.tile([P, SLOTS * OUT], F32, name="ost", tag="ost%d" % (i % NO))
            accs = []
            for s in range(SLOTS):
                acc = psum.tile([P, OUT], F32, name="acc", tag="acc%d" % s)
                for g in range(2):
                    c0 = (s * 2 + g) * P
                    nc.tensor.matmul_mx(
                        out=acc[:],
                        lhsT=xc[:, c0 : c0 + P].bitcast(FP8X4),
                        lhsT_scale=xsc[:, c0 : c0 + P],
                        rhs=w_codes[:, g * OUT : (g + 1) * OUT].bitcast(FP8X4),
                        rhs_scale=w_scales[:, g * OUT : (g + 1) * OUT],
                        start=(g == 0),
                        stop=(g == 1),
                    )
                accs.append(acc)
            for s in range(SLOTS):
                cols = slice(s * OUT, (s + 1) * OUT)
                nc.vector.tensor_tensor(out=ost[:, cols], in0=accs[s][:], in1=bias_bc[:], op=ADD)
                if i >= FINE:
                    nc.sync.dma_start(out=og[i][:, cols], in_=ost[:, cols])
            if i < FINE:
                nc.gpsimd.dma_start(out=og[i], in_=ost[:])

        transposes(0)
        weight_half(0)
        weight_half(1)
        quant_w(0)
        transposes(1)
        quant_w(1)
        quant_x(0, 4)
        quant_x(1, 1)
        for j in range(2, GROUPS + 2):
            if j < GROUPS:
                transposes(j)
            multiply(j - 2)
            if j < GROUPS:
                quant_x(j, 1)
